import numpy as np
import ml_dtypes


def mxq(x, axis, fmt="e4m3"):
    dtype, down = {"e4m3": (ml_dtypes.float8_e4m3fn, 7), "e5m2": (ml_dtypes.float8_e5m2, 14)}[fmt]
    v = np.moveaxis(np.asarray(x, np.float32).astype(ml_dtypes.bfloat16).astype(np.float64), axis, -1)
    blocks = v.reshape(v.shape[:-1] + (-1, 32))
    amax = np.abs(blocks).max(-1, keepdims=True)
    byte = np.maximum(np.where(amax > 0, np.frexp(amax)[1] - 1 + 127, 0) - down, 1)
    scale = np.exp2(byte - 127.0)
    codes = (blocks / scale).astype(np.float32).astype(dtype).astype(np.float64)
    return np.moveaxis((codes * scale).reshape(v.shape), -1, axis)


WIDE = False


def mx_kscale(k):
    if not WIDE:
        return np.ones(k)
    levels = np.array([10, -10, 5, -5, 0])
    if k % 512:
        return np.exp2(np.random.permutation(np.resize(levels, k // 32))).repeat(32)
    a = np.empty((k // 512, 16))
    for p in range(k // 512):
        a[p, :8] = np.random.permutation(np.resize(levels, 8))
        for g in range(8):
            far = levels[np.abs(levels - a[p, g]) >= 10]
            a[p, g + 8] = far[np.random.randint(len(far))]
    return np.exp2(a.ravel()).repeat(32)


BF16 = ml_dtypes.bfloat16


def bf(x):
    return np.asarray(x, np.float32).astype(BF16)


def f64(x):
    return np.asarray(x).astype(np.float64)


N, D = 2048, 128
NEG_INF = -1e9


def setup_inputs():
    s = mx_kscale(N)
    c = np.exp2(np.round(np.log2(s.mean())))
    x = np.round(np.random.standard_normal((N, D)) * 16.0) / 16.0
    adj = np.random.random((N, N)) + np.log(s)[None, :] / 10.0
    aff = np.random.randint(0, 2, (N, N))
    beta = 2.0 + 4.0 * np.random.random(1)
    return {"x": bf(x * (c / s)[:, None]), "adj": bf(adj), "aff_cropping": bf(aff), "beta": bf(beta)}


def reference(x, adj, aff_cropping, beta):
    x, adj, aff_cropping, beta = f64(x), f64(adj), f64(aff_cropping), f64(beta)
    norm2 = np.sqrt((x * x).sum(axis=1, keepdims=True))
    cos = (x @ x.T) / (norm2 * norm2.T + 1e-7)
    mask = np.where((aff_cropping == 0) | (cos < 0), NEG_INF, 0.0)
    masked = beta[0] * cos + mask + 10.0 * adj
    e = np.exp(masked - masked.max(axis=1, keepdims=True))
    return (mxq(e, 1, "e4m3") @ mxq(x, 0, "e4m3")) / e.sum(axis=1, keepdims=True)

@@ -1,0 +1,301 @@
+from contextlib import ExitStack
+
+import concourse.bass as bass
+import concourse.mybir as mybir
+import concourse.tile as tile
+from concourse.masks import make_identity
+
+F32 = mybir.dt.float32
+BF16 = mybir.dt.bfloat16
+U32 = mybir.dt.uint32
+U8 = mybir.dt.uint8
+FP8X4 = mybir.dt.float8_e4m3fn_x4
+ALU = mybir.AluOpType
+ACT = mybir.ActivationFunctionType
+AX = mybir.AxisListType
+
+N = 2048
+D = 128
+P = 128
+NT = N // P
+FLOPS = 2 * 2 * N * N * D
+EPS = 1.0e-7
+BIG = 1.0e9
+HUGE = 1.0e20
+
+
+def bc(ap, n):
+    return ap.unsqueeze(2).to_broadcast([P, NT, n])
+
+
+def tile_graphattentionlayer_kernel(tc, x, adj, aff_cropping, beta, out):
+    nc = tc.nc
+    with ExitStack() as ctx:
+        const = ctx.enter_context(tc.tile_pool(name="const", bufs=1))
+        io = ctx.enter_context(tc.tile_pool(name="io", bufs=4))
+        upool = ctx.enter_context(tc.tile_pool(name="upool", bufs=3))
+        ampool = ctx.enter_context(tc.tile_pool(name="ampool", bufs=6))
+        work = ctx.enter_context(tc.tile_pool(name="work", bufs=2))
+        keep = ctx.enter_context(tc.tile_pool(name="keep", bufs=1))
+        warm = const.tile([P, 1], F32)
+        nc.vector.memset(warm[:], 1.0)
+        nc.scalar.activation(out=warm[:], in_=warm[:], func=ACT.Sqrt)
+        ident_b = const.tile([P, P], BF16)
+        make_identity(nc, ident_b[:])
+        ident_f = const.tile([P, P], F32)
+        make_identity(nc, ident_f[:])
+
+        xn = const.tile([P, NT, D], BF16)
+        nc.sync.dma_start(out=xn[:], in_=x.rearrange("(b p) d -> p b d", p=P))
+        xq = const.tile([P, 4, 4, D], BF16)
+        nc.sync.dma_start(out=xq[:], in_=x.rearrange("(g p t) d -> p g t d", p=P, t=4))
+        beta_b = const.tile([P, 1], BF16)
+        nc.sync.dma_start(out=beta_b[:], in_=beta.partition_broadcast(P))
+        beta_f = const.tile([P, 1], F32)
+        nc.vector.tensor_copy(out=beta_f[:], in_=beta_b[:])
+
+        xT = const.tile([P, N], BF16)
+        lw = const.tile([P, N], BF16)
+        rw = const.tile([P, N], BF16)
+        xg = const.tile([P, 4, D, 4], BF16, align_bytes=64)
+        x_codes = const.tile([P, 4, D], U32, align_bytes=64)
+        x_scales = const.tile([P, 4, D], U8, align_bytes=64)
+
+        with tc.tile_pool(name="setup", bufs=1) as setup, tc.psum_pool(name="ps_setup", bufs=2) as pss:
+            cl = setup.tile([P, NT, P], BF16)
+            nc.gpsimd.memset(cl[:], 0.0)
+            cr = setup.tile([P, NT, P], BF16)
+            nc.gpsimd.memset(cr[:], 0.0)
+            for h in range(4):
+                pt = pss.tile([P, 4, P], BF16)
+                for q in range(4):
+                    nc.tensor.transpose(pt[:, q, :], xn[:, 4 * h + q, :], ident_b[:])
+                nc.scalar.copy(
+                    out=xT[:, 512 * h : 512 * (h + 1)], in_=pt[:].rearrange("p q i -> p (q i)")
+                )
+            sq = setup.tile([P, NT, D], F32)
+            n2 = setup.tile([P, NT], F32)
+            n0 = setup.tile([P, NT], F32)
+            rn0 = setup.tile([P, NT], F32)
+            n1 = setup.tile([P, NT], F32)
+            r = setup.tile([P, NT], F32)
+            s = setup.tile([P, NT], F32)
+            v = setup.tile([P, NT], F32)
+            qq = setup.tile([P, NT], F32)
+            nc.vector.tensor_tensor(out=sq[:, 0:8, :], in0=xn[:, 0:8, :], in1=xn[:, 0:8, :], op=ALU.mult)
+            nc.vector.tensor_reduce(out=n2[:, 0:8], in_=sq[:, 0:8, :], axis=AX.X, op=ALU.add)
+            for b in range(8, NT):
+                nc.scalar.activation(
+                    out=sq[:, b, :], in_=xn[:, b, :], func=ACT.Square, accum_out=n2[:, b : b + 1]
+                )
+            nc.vector.tensor_scalar_max(out=n2[:], in0=n2[:], scalar1=1.0e-20)
+            nc.scalar.activation(out=n0[:], in_=n2[:], func=ACT.Sqrt)
+            nc.vector.reciprocal(out=rn0[:], in_=n0[:])
+            nc.vector.tensor_tensor(out=n1[:], in0=n2[:], in1=rn0[:], op=ALU.mult)
+            nc.vector.tensor_tensor(out=n1[:], in0=n1[:], in1=n0[:], op=ALU.add)
+            nc.vector.tensor_scalar_mul(out=n1[:], in0=n1[:], scalar1=0.5)
+            nc.vector.reciprocal(out=r[:], in_=n1[:])
+            nc.vector.tensor_scalar(
+                out=s[:], in0=r[:], scalar1=beta_f[:, 0:1], scalar2=None, op0=ALU.mult
+            )
+            nc.vector.tensor_tensor(out=qq[:], in0=r[:], in1=r[:], op=ALU.mult)
+            nc.vector.scalar_tensor_tensor(
+                out=v[:], in0=s[:], scalar=-EPS, in1=r[:], op0=ALU.mult, op1=ALU.mult
+            )
+            cr9 = cr[:, :, 0:9].rearrange("p b (a c) -> p b a c", c=3)
+            cr4 = cr[:, :, 9:13].rearrange("p b (a c) -> p b a c", c=2)
+            s1 = setup.tile([P, NT], F32)
+            s2 = setup.tile([P, NT], F32)
+            r1 = setup.tile([P, NT], F32)
+            r2 = setup.tile([P, NT], F32)
+            v1 = setup.tile([P, NT], F32)
+            q1 = setup.tile([P, NT], F32)
+            nc.vector.tensor_copy(out=cl[:, :, 0:3], in_=bc(s[:], 3))
+            nc.vector.tensor_copy(out=cr9[:, :, :, 0], in_=bc(r[:], 3))
+            nc.vector.tensor_copy(out=cl[:, :, 9:11], in_=bc(v[:], 2))
+            nc.vector.tensor_copy(out=cr4[:, :, :, 0], in_=bc(qq[:], 2))
+            nc.vector.tensor_tensor(out=s1[:], in0=s[:], in1=cl[:, :, 0], op=ALU.subtract)
+            nc.vector.tensor_tensor(out=r1[:], in0=r[:], in1=cr[:, :, 0], op=ALU.subtract)
+            nc.vector.tensor_tensor(out=v1[:], in0=v[:], in1=cl[:, :, 9], op=ALU.subtract)
+            nc.vector.tensor_tensor(out=q1[:], in0=qq[:], in1=cr[:, :, 9], op=ALU.subtract)
+            nc.vector.tensor_copy(out=cl[:, :, 3:6], in_=bc(s1[:], 3))
+            nc.vector.tensor_copy(out=cr9[:, :, :, 1], in_=bc(r1[:], 3))
+            nc.vector.tensor_copy(out=cl[:, :, 11:13], in_=bc(v1[:], 2))
+            nc.vector.tensor_copy(out=cr4[:, :, :, 1], in_=bc(q1[:], 2))
+            nc.vector.tensor_tensor(out=s2[:], in0=s1[:], in1=cl[:, :, 3], op=ALU.subtract)
+            nc.vector.tensor_tensor(out=r2[:], in0=r1[:], in1=cr[:, :, 1], op=ALU.subtract)
+            nc.vector.tensor_copy(out=cl[:, :, 6:9], in_=bc(s2[:], 3))
+            nc.vector.tensor_copy(out=cr9[:, :, :, 2], in_=bc(r2[:], 3))
+            jobs = ((cl, lw, 0), (cr, rw, 0), (cr, rw, 1), (cr, rw, 2), (cr, rw, 3), (cl, lw, 1), (cl, lw, 2), (cl, lw, 3))
+            for k, (src, dst, h) in enumerate(jobs):
+                pt = pss.tile([P, 4, P], BF16)
+                for q in range(4):
+                    nc.tensor.transpose(pt[:, q, :], src[:, 4 * h + q, :], ident_b[:])
+                if k % 2 == 0:
+                    nc.vector.tensor_copy(
+                        out=dst[:, 512 * h : 512 * (h + 1)], in_=pt[:].rearrange("p q i -> p (q i)")
+                    )
+                else:
+                    nc.scalar.copy(
+                        out=dst[:, 512 * h : 512 * (h + 1)], in_=pt[:].rearrange("p q i -> p (q i)")
+                    )
+
+            nc.scalar.copy(out=xg[:], in_=xq[:].rearrange("p g t d -> p g d t"))
+            nc.vector.quantize_mx(
+                out=x_codes[:].rearrange("p g d -> p (g d)").bitcast(FP8X4),
+                scales=x_scales[:].rearrange("p g d -> p (g d)"),
+                in_=xg[:].rearrange("p g d t -> p (g d t)"),
+            )
+
+        psg = ctx.enter_context(tc.psum_pool(name="psg", bufs=3))
+        psw = ctx.enter_context(tc.psum_pool(name="psw", bufs=2))
+        pst = ctx.enter_context(tc.psum_pool(name="pst", bufs=2))
+        pso = ctx.enter_context(tc.psum_pool(name="pso", bufs=1))
+
+        panels = []
+        for it in range(NT):
+            rows = slice(it * P, (it + 1) * P)
+            up0 = it * P
+            adj_t = io.tile([P, N], BF16)
+            nc.sync.dma_start(out=adj_t[:], in_=adj[rows, :])
+            aff_t = io.tile([P, N], BF16)
+            nc.sync.dma_start(out=aff_t[:], in_=aff_cropping[rows, :])
+
+            u = upool.tile([P, N], BF16)
+            nc.scalar.activation(out=u[:], in_=aff_t[:], func=ACT.Copy, bias=-BIG, scale=BIG)
+            am = ampool.tile([P, N], BF16)
+            nc.vector.tensor_tensor(out=am[:], in0=adj_t[:], in1=u[:], op=ALU.add)
+
+            panel = keep.tile([P, N - up0], F32, name="panel%d" % it)
+            panels.append(panel)
+            for c in range(it // 4, 4):
+                a0 = max(512 * c, up0)
+                a1 = 512 * (c + 1)
+                w = psw.tile([P, 512], F32)
+                nc.tensor.matmul(
+                    out=w[:, : a1 - a0], lhsT=lw[:, rows], rhs=rw[:, a0:a1], start=True, stop=True
+                )
+                nc.scalar.copy(out=panel[:, a0 - up0 : a1 - up0], in_=w[:, : a1 - a0])
+
+            z = work.tile([P, N], F32)
+            gts = {}
+
+            def fill(c):
+                nlow = min(max(it - 4 * c, 0), 4)
+                lo = nlow * P
+                g = psg.tile([P, 512], F32, name="g")
+                for q in range(nlow):
+                    jb = 4 * c + q
+                    nc.tensor.transpose(
+                        g[:, q * P : (q + 1) * P],
+                        panels[jb][:, (it - jb) * P : (it - jb + 1) * P],
+                        ident_f[:],
+                    )
+                if nlow < 4:
+                    nc.tensor.matmul(
+                        out=g[:, lo:], lhsT=xT[:, rows], rhs=xT[:, 512 * c + lo : 512 * (c + 1)],
+                        start=True, stop=True,
+                    )
+                gts[c] = g
+
+            def seg_of(c):
+                lo = min(max(it - 4 * c, 0), 4) * P
+                return panel[:, 512 * c + lo - up0 : 512 * (c + 1) - up0], lo
+
+            def op_y(c):
+                seg, lo = seg_of(c)
+                nc.vector.tensor_tensor(out=seg, in0=gts[c][:, lo:], in1=seg, op=ALU.mult)
+
+            def op_s(c):
+                seg, lo = seg_of(c)
+                nc.vector.scalar_tensor_tensor(
+                    out=seg, in0=gts[c][:, lo:], scalar=HUGE, in1=seg, op0=ALU.mult, op1=ALU.min
+                )
+
+            def op_low(c):
+                lo = min(max(it - 4 * c, 0), 4) * P
+                nc.vector.scalar_tensor_tensor(
+                    out=z[:, 512 * c : 512 * c + lo], in0=am[:, 512 * c : 512 * c + lo], scalar=10.0,
+                    in1=gts[c][:, :lo], op0=ALU.mult, op1=ALU.add,
+                )
+
+            cb = it // 4
+            ups = list(range(cb, 4))
+            lows = list(range(0, cb + 1)) if it % 4 else list(range(0, cb))
+            fill(ups[0])
+            if len(ups) > 1:
+                fill(ups[1])
+            op_y(ups[0])
+            for k in range(1, len(ups)):
+                op_y(ups[k])
+                op_s(ups[k - 1])
+                if ups[k - 1] in lows:
+                    op_low(ups[k - 1])
+                if k + 1 < len(ups):
+                    fill(ups[k + 1])
+            rest = [c for c in lows if c not in ups]
+            if rest:
+                fill(rest[0])
+                op_low(rest[0])
+            op_s(ups[-1])
+            if ups[-1] in lows:
+                op_low(ups[-1])
+            for c in rest[1:]:
+                fill(c)
+                op_low(c)
+            nc.vector.scalar_tensor_tensor(
+                out=z[:, up0:], in0=am[:, up0:], scalar=10.0, in1=panel[:], op0=ALU.mult, op1=ALU.add
+            )
+            negm = work.tile([P, 1], F32)
+            nc.vector.tensor_reduce(out=negm[:], in_=z[:], axis=AX.X, op=ALU.max, negate=True)
+
+            e = work.tile([P, N], BF16)
+            ssum4 = work.tile([P, 4], F32)
+            eg = work.tile([P, 4, P, 4], BF16, align_bytes=64)
+            for gq in range(4):
+                cols = slice(512 * gq, 512 * (gq + 1))
+                nc.scalar.activation(
+                    out=e[:, cols], in_=z[:, cols], func=ACT.Exp, bias=negm[:, 0:1], scale=1.0,
+                    accum_out=ssum4[:, gq : gq + 1],
+                )
+                pt = pst.tile([P, 4, P], BF16)
+                for t in range(4):
+                    nc.tensor.transpose(pt[:, t, :], e[:, 512 * gq + t : 512 * (gq + 1) : 4], ident_b[:])
+                if it == NT - 1:
+                    nc.vector.tensor_copy(out=eg[:, gq, :, :], in_=pt[:].rearrange("p t i -> p i t"))
+                else:
+                    nc.scalar.copy(out=eg[:, gq, :, :], in_=pt[:].rearrange("p t i -> p i t"))
+            e_codes = work.tile([P, 4, P], U32, align_bytes=64)
+            e_scales = work.tile([P, 4, P], U8, align_bytes=64)
+            if it == NT - 1:
+                for gq in range(4):
+                    nc.vector.quantize_mx(
+                        out=e_codes[:, gq, :].bitcast(FP8X4),
+                        scales=e_scales[:, gq, :],
+                        in_=eg[:, gq, :, :].rearrange("p i t -> p (i t)"),
+                    )
+            else:
+                nc.vector.quantize_mx(
+                    out=e_codes[:].rearrange("p g i -> p (g i)").bitcast(FP8X4),
+                    scales=e_scales[:].rearrange("p g i -> p (g i)"),
+                    in_=eg[:].rearrange("p g i t -> p (g i t)"),
+                )
+            acc = pso.tile([P, D], F32)
+            for gq in range(4):
+                nc.tensor.matmul_mx(
+                    out=acc[:],
+                    lhsT=e_codes[:, gq, :].bitcast(FP8X4),
+                    lhsT_scale=e_scales[:, gq, :],
+                    rhs=x_codes[:, gq, :].bitcast(FP8X4),
+                    rhs_scale=x_scales[:, gq, :],
+                    start=(gq == 0),
+                    stop=(gq == 3),
+                )
+            ssum = work.tile([P, 1], F32)
+            sjunk = work.tile([P, 4], F32)
+            nc.scalar.activation(out=sjunk[:], in_=ssum4[:], func=ACT.Copy, accum_out=ssum[:, 0:1])
+            rs = work.tile([P, 1], F32)
+            nc.vector.reciprocal(out=rs[:], in_=ssum[:])
+            o = work.tile([P, D], F32)
+            nc.scalar.activation(out=o[:], in_=acc[:], func=ACT.Copy, scale=rs[:, 0:1])
+            nc.sync.dma_start(out=out[rows, :], in_=o[:])

@@ -258,13 +258,15 @@ def tile_graphattentionlayer_kernel(tc, x, adj, aff_cropping, beta, out):
                     out=e[:, cols], in_=z[:, cols], func=ACT.Exp, bias=negm[:, 0:1], scale=1.0,
                     accum_out=ssum4[:, gq : gq + 1],
                 )
-                pt = pst.tile([P, 4, P], BF16)
-                for t in range(4):
-                    nc.tensor.transpose(pt[:, t, :], e[:, 512 * gq + t : 512 * (gq + 1) : 4], ident_b[:])
+                ew = e[:].bitcast(F32)
+                pt = pst.tile([P, 2, P], F32)
+                for u in range(2):
+                    nc.tensor.transpose(pt[:, u, :], ew[:, 256 * gq + u : 256 * (gq + 1) : 2], ident_f[:])
+                eg_w = eg[:, gq, :, :].bitcast(F32)
                 if it == NT - 1:
-                    nc.vector.tensor_copy(out=eg[:, gq, :, :], in_=pt[:].rearrange("p t i -> p i t"))
+                    nc.vector.tensor_copy(out=eg_w, in_=pt[:].rearrange("p u i -> p i u"))
                 else:
-                    nc.scalar.copy(out=eg[:, gq, :, :], in_=pt[:].rearrange("p t i -> p i t"))
+                    nc.scalar.copy(out=eg_w, in_=pt[:].rearrange("p u i -> p i u"))
             e_codes = work.tile([P, 4, P], U32, align_bytes=64)
             e_scales = work.tile([P, 4, P], U8, align_bytes=64)
             if it == NT - 1:

@@ -140,7 +140,11 @@ def tile_graphattentionlayer_kernel(tc, x, adj, aff_cropping, beta, out):
                         out=dst[:, 512 * h : 512 * (h + 1)], in_=pt[:].rearrange("p q i -> p (q i)")
                     )
 
-            nc.scalar.copy(out=xg[:], in_=xq[:].rearrange("p g t d -> p g d t"))
+            for gq in range(4):
+                nc.scalar.copy(
+                    out=xg[:, gq, :, :].rearrange("p d (u v) -> p d u v", u=2),
+                    in_=xq[:, gq, :, :].rearrange("p (v u) d -> p d u v", u=2),
+                )
             nc.vector.quantize_mx(
                 out=x_codes[:].rearrange("p g d -> p (g d)").bitcast(FP8X4),
                 scales=x_scales[:].rearrange("p g d -> p (g d)"),
@@ -255,13 +259,14 @@ def tile_graphattentionlayer_kernel(tc, x, adj, aff_cropping, beta, out):
             for gq in range(4):
                 cols = slice(512 * gq, 512 * (gq + 1))
                 nc.scalar.activation(
-                    out=e[:, cols], in_=z[:, cols], func=ACT.Exp, bias=negm[:, 0:1], scale=1.0,
+                    out=e[:, cols].rearrange("p (u w) -> p u w", u=2),
+                    in_=z[:, cols].rearrange("p (w u) -> p u w", u=2), func=ACT.Exp, bias=negm[:, 0:1], scale=1.0,
                     accum_out=ssum4[:, gq : gq + 1],
                 )
                 ew = e[:].bitcast(F32)
                 pt = pst.tile([P, 2, P], F32)
                 for u in range(2):
-                    nc.tensor.transpose(pt[:, u, :], ew[:, 256 * gq + u : 256 * (gq + 1) : 2], ident_f[:])
+                    nc.tensor.transpose(pt[:, u, :], ew[:, 256 * gq + P * u : 256 * gq + P * (u + 1)], ident_f[:])
                 eg_w = eg[:, gq, :, :].bitcast(F32)
                 if it == NT - 1:
                     nc.vector.tensor_copy(out=eg_w, in_=pt[:].rearrange("p u i -> p i u"))

@@ -32,14 +32,17 @@ def tile_graphattentionlayer_kernel(tc, x, adj, aff_cropping, beta, out):
     nc = tc.nc
     with ExitStack() as ctx:
         const = ctx.enter_context(tc.tile_pool(name="const", bufs=1))
+        adjpool = ctx.enter_context(tc.tile_pool(name="adjpool", bufs=7))
         io = ctx.enter_context(tc.tile_pool(name="io", bufs=4))
-        upool = ctx.enter_context(tc.tile_pool(name="upool", bufs=3))
-        ampool = ctx.enter_context(tc.tile_pool(name="ampool", bufs=6))
+        ampool = ctx.enter_context(tc.tile_pool(name="ampool", bufs=9))
         work = ctx.enter_context(tc.tile_pool(name="work", bufs=2))
         keep = ctx.enter_context(tc.tile_pool(name="keep", bufs=1))
+        tbpool = ctx.enter_context(tc.tile_pool(name="tbpool", bufs=3))
         warm = const.tile([P, 1], F32)
         nc.vector.memset(warm[:], 1.0)
         nc.scalar.activation(out=warm[:], in_=warm[:], func=ACT.Sqrt)
+        minus1 = const.tile([P, 1], F32)
+        nc.gpsimd.memset(minus1[:], -1.0)
         ident_b = const.tile([P, P], BF16)
         make_identity(nc, ident_b[:])
         ident_f = const.tile([P, P], F32)
@@ -47,7 +50,7 @@ def tile_graphattentionlayer_kernel(tc, x, adj, aff_cropping, beta, out):
 
         xn = const.tile([P, NT, D], BF16)
         nc.sync.dma_start(out=xn[:], in_=x.rearrange("(b p) d -> p b d", p=P))
-        xq = const.tile([P, 4, 4, D], BF16)
+        xq = work.tile([P, 4, 4, D], BF16, tag="e")
         nc.sync.dma_start(out=xq[:], in_=x.rearrange("(g p t) d -> p g t d", p=P, t=4))
         beta_b = const.tile([P, 1], BF16)
         nc.sync.dma_start(out=beta_b[:], in_=beta.partition_broadcast(P))
@@ -151,35 +154,53 @@ def tile_graphattentionlayer_kernel(tc, x, adj, aff_cropping, beta, out):
                 in_=xg[:].rearrange("p g d t -> p (g d t)"),
             )
 
-        psg = ctx.enter_context(tc.psum_pool(name="psg", bufs=3))
+        psg = ctx.enter_context(tc.psum_pool(name="psg", bufs=2))
+        psz = ctx.enter_context(tc.psum_pool(name="psz", bufs=2))
         psw = ctx.enter_context(tc.psum_pool(name="psw", bufs=2))
         pst = ctx.enter_context(tc.psum_pool(name="pst", bufs=2))
-        pso = ctx.enter_context(tc.psum_pool(name="pso", bufs=1))
 
         panels = []
         for it in range(NT):
             rows = slice(it * P, (it + 1) * P)
             up0 = it * P
-            adj_t = io.tile([P, N], BF16)
+            adj_t = adjpool.tile([P, N], BF16)
             nc.sync.dma_start(out=adj_t[:], in_=adj[rows, :])
             aff_t = io.tile([P, N], BF16)
             nc.sync.dma_start(out=aff_t[:], in_=aff_cropping[rows, :])
 
-            u = upool.tile([P, N], BF16)
-            nc.scalar.activation(out=u[:], in_=aff_t[:], func=ACT.Copy, bias=-BIG, scale=BIG)
+            a0 = 512 if it >= 4 else 0
             am = ampool.tile([P, N], BF16)
-            nc.vector.tensor_tensor(out=am[:], in0=adj_t[:], in1=u[:], op=ALU.add)
+            if it >= 10:
+                nc.vector.tensor_scalar(
+                    out=am[:, a0:], in0=aff_t[:, a0:], scalar1=BIG, scalar2=-BIG, op0=ALU.mult, op1=ALU.add
+                )
+            else:
+                nc.scalar.activation(out=am[:, a0:], in_=aff_t[:, a0:], func=ACT.Copy, bias=-BIG, scale=BIG)
+            nc.vector.tensor_tensor(out=am[:, a0:], in0=adj_t[:, a0:], in1=am[:, a0:], op=ALU.add)
+            if a0:
+                bt = psw.tile([P, 2, 4, P], BF16, tag="w")
+                for j, src in enumerate((adj_t, aff_t)):
+                    for q in range(4):
+                        nc.tensor.transpose(bt[:, j, q, :], src[:, q * P : (q + 1) * P], ident_b[:])
+                tb = tbpool.tile([P, 2, 512], F32)
+                nc.scalar.activation(
+                    out=tb[:, 0, :], in_=bt[:, 0, :, :].rearrange("p q i -> p (q i)"), func=ACT.Copy, scale=10.0
+                )
+                nc.scalar.activation(
+                    out=tb[:, 1, :], in_=bt[:, 1, :, :].rearrange("p q i -> p (q i)"), func=ACT.Copy,
+                    bias=-10.0 * BIG, scale=10.0 * BIG,
+                )
 
             panel = keep.tile([P, N - up0], F32, name="panel%d" % it)
             panels.append(panel)
             for c in range(it // 4, 4):
-                a0 = max(512 * c, up0)
-                a1 = 512 * (c + 1)
-                w = psw.tile([P, 512], F32)
+                c0 = max(512 * c, up0)
+                c1 = 512 * (c + 1)
+                w = psw.tile([P, 512], F32, tag="w")
                 nc.tensor.matmul(
-                    out=w[:, : a1 - a0], lhsT=lw[:, rows], rhs=rw[:, a0:a1], start=True, stop=True
+                    out=w[:, : c1 - c0], lhsT=lw[:, rows], rhs=rw[:, c0:c1], start=True, stop=True
                 )
-                nc.scalar.copy(out=panel[:, a0 - up0 : a1 - up0], in_=w[:, : a1 - a0])
+                nc.scalar.copy(out=panel[:, c0 - up0 : c1 - up0], in_=w[:, : c1 - c0])
 
             z = work.tile([P, N], F32)
             gts = {}
@@ -223,9 +244,19 @@ def tile_graphattentionlayer_kernel(tc, x, adj, aff_cropping, beta, out):
                     in1=gts[c][:, :lo], op0=ALU.mult, op1=ALU.add,
                 )
 
+            if a0:
+                zl = psz.tile([P, 512], F32)
+                for q in range(4):
+                    blk = slice(q * P, (q + 1) * P)
+                    srcs = (panels[q][:, (it - q) * P : (it - q + 1) * P], tb[:, 0, blk], tb[:, 1, blk])
+                    for k, src in enumerate(srcs):
+                        nc.tensor.matmul(
+                            out=zl[:, blk], lhsT=src, rhs=ident_f[:], is_transpose=True,
+                            start=(k == 0), stop=(k == 2),
+                        )
             cb = it // 4
             ups = list(range(cb, 4))
-            lows = list(range(0, cb + 1)) if it % 4 else list(range(0, cb))
+            lows = list(range(a0 // 512, cb + 1 if it % 4 else cb))
             fill(ups[0])
             if len(ups) > 1:
                 fill(ups[1])
@@ -251,7 +282,13 @@ def tile_graphattentionlayer_kernel(tc, x, adj, aff_cropping, beta, out):
                 out=z[:, up0:], in0=am[:, up0:], scalar=10.0, in1=panel[:], op0=ALU.mult, op1=ALU.add
             )
             negm = work.tile([P, 1], F32)
-            nc.vector.tensor_reduce(out=negm[:], in_=z[:], axis=AX.X, op=ALU.max, negate=True)
+            if a0:
+                mx = work.tile([P, 2], F32)
+                nc.vector.tensor_reduce(out=mx[:, 0:1], in_=zl[:], axis=AX.X, op=ALU.max)
+                nc.vector.tensor_reduce(out=mx[:, 1:2], in_=z[:, a0:], axis=AX.X, op=ALU.max)
+                nc.vector.tensor_reduce(out=negm[:], in_=mx[:], axis=AX.X, op=ALU.max, negate=True)
+            else:
+                nc.vector.tensor_reduce(out=negm[:], in_=z[:], axis=AX.X, op=ALU.max, negate=True)
 
             e = work.tile([P, N], BF16)
             ssum4 = work.tile([P, 4], F32)
@@ -260,11 +297,11 @@ def tile_graphattentionlayer_kernel(tc, x, adj, aff_cropping, beta, out):
                 cols = slice(512 * gq, 512 * (gq + 1))
                 nc.scalar.activation(
                     out=e[:, cols].rearrange("p (u w) -> p u w", u=2),
-                    in_=z[:, cols].rearrange("p (w u) -> p u w", u=2), func=ACT.Exp, bias=negm[:, 0:1], scale=1.0,
+                    in_=(zl[:] if a0 and gq == 0 else z[:, cols]).rearrange("p (w u) -> p u w", u=2), func=ACT.Exp, bias=negm[:, 0:1], scale=1.0,
                     accum_out=ssum4[:, gq : gq + 1],
                 )
                 ew = e[:].bitcast(F32)
-                pt = pst.tile([P, 2, P], F32)
+                pt = pst.tile([P, 2, P], F32, tag="pt")
                 for u in range(2):
                     nc.tensor.transpose(pt[:, u, :], ew[:, 256 * gq + P * u : 256 * gq + P * (u + 1)], ident_f[:])
                 eg_w = eg[:, gq, :, :].bitcast(F32)
@@ -287,10 +324,11 @@ def tile_graphattentionlayer_kernel(tc, x, adj, aff_cropping, beta, out):
                     scales=e_scales[:].rearrange("p g i -> p (g i)"),
                     in_=eg[:].rearrange("p g i t -> p (g i t)"),
                 )
-            acc = pso.tile([P, D], F32)
+            acc_t = pst.tile([P, 2, P], F32, tag="pt")
+            acc = acc_t[:, 0, :]
             for gq in range(4):
                 nc.tensor.matmul_mx(
-                    out=acc[:],
+                    out=acc,
                     lhsT=e_codes[:, gq, :].bitcast(FP8X4),
                     lhsT_scale=e_scales[:, gq, :],
                     rhs=x_codes[:, gq, :].bitcast(FP8X4),
@@ -302,7 +340,7 @@ def tile_graphattentionlayer_kernel(tc, x, adj, aff_cropping, beta, out):
             sjunk = work.tile([P, 4], F32)
             nc.scalar.activation(out=sjunk[:], in_=ssum4[:], func=ACT.Copy, accum_out=ssum[:, 0:1])
             rs = work.tile([P, 1], F32)
-            nc.vector.reciprocal(out=rs[:], in_=ssum[:])
+            nc.gpsimd.tensor_tensor(out=rs[:], in0=ssum[:], in1=minus1[:], op=ALU.pow)
             o = work.tile([P, D], F32)
-            nc.scalar.activation(out=o[:], in_=acc[:], func=ACT.Copy, scale=rs[:, 0:1])
+            nc.scalar.activation(out=o[:], in_=acc, func=ACT.Copy, scale=rs[:, 0:1])
             nc.sync.dma_start(out=out[rows, :], in_=o[:])

@@ -24,10 +24,6 @@ BIG = 1.0e9
 HUGE = 1.0e20
 
 
-def bc(ap, n):
-    return ap.unsqueeze(2).to_broadcast([P, NT, n])
-
-
 def tile_graphattentionlayer_kernel(tc, x, adj, aff_cropping, beta, out):
     nc = tc.nc
     with ExitStack() as ctx:
@@ -49,24 +45,23 @@ def tile_graphattentionlayer_kernel(tc, x, adj, aff_cropping, beta, out):
         make_identity(nc, ident_f[:])
 
         xn = const.tile([P, NT, D], BF16)
-        nc.sync.dma_start(out=xn[:], in_=x.rearrange("(b p) d -> p b d", p=P))
-        xq = work.tile([P, 4, 4, D], BF16, tag="e")
-        nc.sync.dma_start(out=xq[:], in_=x.rearrange("(g p t) d -> p g t d", p=P, t=4))
+        x_rows = x.rearrange("(b p) d -> p b d", p=P)
+        nc.sync.dma_start(out=xn[:, 0:8, :], in_=x_rows[:, 0:8, :])
+        nc.scalar.dma_start(out=xn[:, 8:NT, :], in_=x_rows[:, 8:NT, :])
         beta_b = const.tile([P, 1], BF16)
         nc.sync.dma_start(out=beta_b[:], in_=beta.partition_broadcast(P))
-        beta_f = const.tile([P, 1], F32)
-        nc.vector.tensor_copy(out=beta_f[:], in_=beta_b[:])
+        beta4 = const.tile([P, 1], F32)
+        nc.vector.tensor_scalar_mul(out=beta4[:], in0=beta_b[:], scalar1=4.0)
 
         xT = const.tile([P, N], BF16)
         lw = const.tile([P, N], BF16)
         rw = const.tile([P, N], BF16)
-        xg = const.tile([P, 4, D, 4], BF16, align_bytes=64)
         x_codes = const.tile([P, 4, D], U32, align_bytes=64)
+        cl = const.tile([P, NT, P], BF16)
+        nc.gpsimd.memset(cl[:], 0.0)
         x_scales = const.tile([P, 4, D], U8, align_bytes=64)
 
-        with tc.tile_pool(name="setup", bufs=1) as setup, tc.psum_pool(name="ps_setup", bufs=2) as pss:
-            cl = setup.tile([P, NT, P], BF16)
-            nc.gpsimd.memset(cl[:], 0.0)
+        with tc.tile_pool(name="setup", bufs=1) as setup, tc.psum_pool(name="ps_setup", bufs=4) as pss:
             cr = setup.tile([P, NT, P], BF16)
             nc.gpsimd.memset(cr[:], 0.0)
             for h in range(4):
@@ -81,10 +76,6 @@ def tile_graphattentionlayer_kernel(tc, x, adj, aff_cropping, beta, out):
             n0 = setup.tile([P, NT], F32)
             rn0 = setup.tile([P, NT], F32)
             n1 = setup.tile([P, NT], F32)
-            r = setup.tile([P, NT], F32)
-            s = setup.tile([P, NT], F32)
-            v = setup.tile([P, NT], F32)
-            qq = setup.tile([P, NT], F32)
             nc.vector.tensor_tensor(out=sq[:, 0:8, :], in0=xn[:, 0:8, :], in1=xn[:, 0:8, :], op=ALU.mult)
             nc.vector.tensor_reduce(out=n2[:, 0:8], in_=sq[:, 0:8, :], axis=AX.X, op=ALU.add)
             for b in range(8, NT):
@@ -96,63 +87,43 @@ def tile_graphattentionlayer_kernel(tc, x, adj, aff_cropping, beta, out):
             nc.vector.reciprocal(out=rn0[:], in_=n0[:])
             nc.vector.tensor_tensor(out=n1[:], in0=n2[:], in1=rn0[:], op=ALU.mult)
             nc.vector.tensor_tensor(out=n1[:], in0=n1[:], in1=n0[:], op=ALU.add)
-            nc.vector.tensor_scalar_mul(out=n1[:], in0=n1[:], scalar1=0.5)
-            nc.vector.reciprocal(out=r[:], in_=n1[:])
-            nc.vector.tensor_scalar(
-                out=s[:], in0=r[:], scalar1=beta_f[:, 0:1], scalar2=None, op0=ALU.mult
-            )
-            nc.vector.tensor_tensor(out=qq[:], in0=r[:], in1=r[:], op=ALU.mult)
-            nc.vector.scalar_tensor_tensor(
-                out=v[:], in0=s[:], scalar=-EPS, in1=r[:], op0=ALU.mult, op1=ALU.mult
-            )
-            cr9 = cr[:, :, 0:9].rearrange("p b (a c) -> p b a c", c=3)
-            cr4 = cr[:, :, 9:13].rearrange("p b (a c) -> p b a c", c=2)
-            s1 = setup.tile([P, NT], F32)
-            s2 = setup.tile([P, NT], F32)
-            r1 = setup.tile([P, NT], F32)
-            r2 = setup.tile([P, NT], F32)
-            v1 = setup.tile([P, NT], F32)
-            q1 = setup.tile([P, NT], F32)
-            nc.vector.tensor_copy(out=cl[:, :, 0:3], in_=bc(s[:], 3))
-            nc.vector.tensor_copy(out=cr9[:, :, :, 0], in_=bc(r[:], 3))
-            nc.vector.tensor_copy(out=cl[:, :, 9:11], in_=bc(v[:], 2))
-            nc.vector.tensor_copy(out=cr4[:, :, :, 0], in_=bc(qq[:], 2))
-            nc.vector.tensor_tensor(out=s1[:], in0=s[:], in1=cl[:, :, 0], op=ALU.subtract)
-            nc.vector.tensor_tensor(out=r1[:], in0=r[:], in1=cr[:, :, 0], op=ALU.subtract)
-            nc.vector.tensor_tensor(out=v1[:], in0=v[:], in1=cl[:, :, 9], op=ALU.subtract)
-            nc.vector.tensor_tensor(out=q1[:], in0=qq[:], in1=cr[:, :, 9], op=ALU.subtract)
-            nc.vector.tensor_copy(out=cl[:, :, 3:6], in_=bc(s1[:], 3))
-            nc.vector.tensor_copy(out=cr9[:, :, :, 1], in_=bc(r1[:], 3))
-            nc.vector.tensor_copy(out=cl[:, :, 11:13], in_=bc(v1[:], 2))
-            nc.vector.tensor_copy(out=cr4[:, :, :, 1], in_=bc(q1[:], 2))
-            nc.vector.tensor_tensor(out=s2[:], in0=s1[:], in1=cl[:, :, 3], op=ALU.subtract)
-            nc.vector.tensor_tensor(out=r2[:], in0=r1[:], in1=cr[:, :, 1], op=ALU.subtract)
-            nc.vector.tensor_copy(out=cl[:, :, 6:9], in_=bc(s2[:], 3))
-            nc.vector.tensor_copy(out=cr9[:, :, :, 2], in_=bc(r2[:], 3))
-            jobs = ((cl, lw, 0), (cr, rw, 0), (cr, rw, 1), (cr, rw, 2), (cr, rw, 3), (cl, lw, 1), (cl, lw, 2), (cl, lw, 3))
-            for k, (src, dst, h) in enumerate(jobs):
+            fac = setup.tile([P, 4, NT], F32)
+            s, r, v, qq = (fac[:, j, :] for j in range(4))
+            nc.vector.reciprocal(out=r, in_=n1[:])
+            nc.vector.tensor_scalar(out=s, in0=r, scalar1=beta4[:, 0:1], scalar2=None, op0=ALU.mult)
+            nc.vector.tensor_tensor(out=qq, in0=r, in1=r, op=ALU.mult)
+            nc.vector.scalar_tensor_tensor(out=v, in0=s, scalar=-4.0 * EPS, in1=r, op0=ALU.mult, op1=ALU.mult)
+            pcs = setup.tile([P, 3, 4, NT], BF16)
+            d1 = setup.tile([P, 4, NT], F32)
+            d2 = setup.tile([P, 4, NT], F32)
+            nc.vector.tensor_copy(out=pcs[:, 0, :, :], in_=fac[:])
+            nc.vector.tensor_tensor(out=d1[:], in0=fac[:], in1=pcs[:, 0, :, :], op=ALU.subtract)
+            nc.vector.tensor_copy(out=pcs[:, 1, :, :], in_=d1[:])
+            nc.vector.tensor_tensor(out=d2[:], in0=d1[:], in1=pcs[:, 1, :, :], op=ALU.subtract)
+            nc.vector.tensor_copy(out=pcs[:, 2, :, :], in_=d2[:])
+            for dst, j, left in ((cl, 0, True), (cr, 1, False), (cl, 2, True), (cr, 3, False)):
+                k0, pn = (0, 3) if j < 2 else (9, 2)
+                piece = pcs[:, 0:pn, j, :].rearrange("p a b -> p b a")
+                if left:
+                    piece = piece.unsqueeze(3).to_broadcast([P, NT, pn, pn])
+                else:
+                    piece = piece.unsqueeze(2).to_broadcast([P, NT, pn, pn])
+                nc.vector.tensor_copy(
+                    out=dst[:, :, k0 : k0 + pn * pn].rearrange("p b (a c) -> p b a c", c=pn), in_=piece
+                )
+            for h in range(5):
+                src, dst, h4 = (cl, lw, 0) if h == 0 else (cr, rw, h - 1)
                 pt = pss.tile([P, 4, P], BF16)
                 for q in range(4):
-                    nc.tensor.transpose(pt[:, q, :], src[:, 4 * h + q, :], ident_b[:])
-                if k % 2 == 0:
+                    nc.tensor.transpose(pt[:, q, :], src[:, 4 * h4 + q, :], ident_b[:])
+                if h % 2 == 0:
                     nc.vector.tensor_copy(
-                        out=dst[:, 512 * h : 512 * (h + 1)], in_=pt[:].rearrange("p q i -> p (q i)")
+                        out=dst[:, 512 * h4 : 512 * (h4 + 1)], in_=pt[:].rearrange("p q i -> p (q i)")
                     )
                 else:
                     nc.scalar.copy(
-                        out=dst[:, 512 * h : 512 * (h + 1)], in_=pt[:].rearrange("p q i -> p (q i)")
+                        out=dst[:, 512 * h4 : 512 * (h4 + 1)], in_=pt[:].rearrange("p q i -> p (q i)")
                     )
-
-            for gq in range(4):
-                nc.scalar.copy(
-                    out=xg[:, gq, :, :].rearrange("p d (u v) -> p d u v", u=2),
-                    in_=xq[:, gq, :, :].rearrange("p (v u) d -> p d u v", u=2),
-                )
-            nc.vector.quantize_mx(
-                out=x_codes[:].rearrange("p g d -> p (g d)").bitcast(FP8X4),
-                scales=x_scales[:].rearrange("p g d -> p (g d)"),
-                in_=xg[:].rearrange("p g d t -> p (g d t)"),
-            )
 
         psg = ctx.enter_context(tc.psum_pool(name="psg", bufs=2))
         psz = ctx.enter_context(tc.psum_pool(name="psz", bufs=2))
@@ -170,7 +141,7 @@ def tile_graphattentionlayer_kernel(tc, x, adj, aff_cropping, beta, out):
 
             a0 = 512 if it >= 4 else 0
             am = ampool.tile([P, N], BF16)
-            if it >= 10:
+            if it < 2 or it >= 10:
                 nc.vector.tensor_scalar(
                     out=am[:, a0:], in0=aff_t[:, a0:], scalar1=BIG, scalar2=-BIG, op0=ALU.mult, op1=ALU.add
                 )
@@ -191,6 +162,14 @@ def tile_graphattentionlayer_kernel(tc, x, adj, aff_cropping, beta, out):
                     bias=-10.0 * BIG, scale=10.0 * BIG,
                 )
 
+            if it % 4 == 2 and it < 12:
+                h4 = it // 4 + 1
+                lt = psw.tile([P, 4, P], BF16, tag="w")
+                for q in range(4):
+                    nc.tensor.transpose(lt[:, q, :], cl[:, 4 * h4 + q, :], ident_b[:])
+                nc.scalar.copy(
+                    out=lw[:, 512 * h4 : 512 * (h4 + 1)], in_=lt[:].rearrange("p q i -> p (q i)")
+                )
             panel = keep.tile([P, N - up0], F32, name="panel%d" % it)
             panels.append(panel)
             for c in range(it // 4, 4):
@@ -290,9 +269,23 @@ def tile_graphattentionlayer_kernel(tc, x, adj, aff_cropping, beta, out):
             else:
                 nc.vector.tensor_reduce(out=negm[:], in_=z[:], axis=AX.X, op=ALU.max, negate=True)
 
-            e = work.tile([P, N], BF16)
+            if it == 0:
+                xq = work.tile([P, 4, 4, D], BF16, tag="e")
+                nc.sync.dma_start(out=xq[:], in_=x.rearrange("(g p t) d -> p g t d", p=P, t=4))
+                xg = work.tile([P, 4, D, 4], BF16, tag="eg", align_bytes=64)
+                for gq in range(4):
+                    nc.scalar.copy(
+                        out=xg[:, gq, :, :].rearrange("p d (u v) -> p d u v", u=2),
+                        in_=xq[:, gq, :, :].rearrange("p (v u) d -> p d u v", u=2),
+                    )
+                nc.vector.quantize_mx(
+                    out=x_codes[:].rearrange("p g d -> p (g d)").bitcast(FP8X4),
+                    scales=x_scales[:].rearrange("p g d -> p (g d)"),
+                    in_=xg[:].rearrange("p g d t -> p (g d t)"),
+                )
+            e = work.tile([P, N], BF16, tag="e")
             ssum4 = work.tile([P, 4], F32)
-            eg = work.tile([P, 4, P, 4], BF16, align_bytes=64)
+            eg = work.tile([P, 4, P, 4], BF16, tag="eg", align_bytes=64)
             for gq in range(4):
                 cols = slice(512 * gq, 512 * (gq + 1))
                 nc.scalar.activation(

@@ -141,7 +141,7 @@ def tile_graphattentionlayer_kernel(tc, x, adj, aff_cropping, beta, out):
 
             a0 = 512 if it >= 4 else 0
             am = ampool.tile([P, N], BF16)
-            if it < 2 or it >= 10:
+            if it < 4:
                 nc.vector.tensor_scalar(
                     out=am[:, a0:], in0=aff_t[:, a0:], scalar1=BIG, scalar2=-BIG, op0=ALU.mult, op1=ALU.add
                 )
@@ -286,22 +286,26 @@ def tile_graphattentionlayer_kernel(tc, x, adj, aff_cropping, beta, out):
             e = work.tile([P, N], BF16, tag="e")
             ssum4 = work.tile([P, 4], F32)
             eg = work.tile([P, 4, P, 4], BF16, tag="eg", align_bytes=64)
-            for gq in range(4):
-                cols = slice(512 * gq, 512 * (gq + 1))
-                nc.scalar.activation(
-                    out=e[:, cols].rearrange("p (u w) -> p u w", u=2),
-                    in_=(zl[:] if a0 and gq == 0 else z[:, cols]).rearrange("p (w u) -> p u w", u=2), func=ACT.Exp, bias=negm[:, 0:1], scale=1.0,
-                    accum_out=ssum4[:, gq : gq + 1],
-                )
-                ew = e[:].bitcast(F32)
-                pt = pst.tile([P, 2, P], F32, tag="pt")
-                for u in range(2):
-                    nc.tensor.transpose(pt[:, u, :], ew[:, 256 * gq + P * u : 256 * gq + P * (u + 1)], ident_f[:])
-                eg_w = eg[:, gq, :, :].bitcast(F32)
+            ew = e[:].bitcast(F32)
+            step = 1 if it == NT - 1 else 2
+            for g0 in range(0, 4, step):
+                pt = pst.tile([P, 2, 2, P], F32, tag="pt")
+                for gq in range(g0, g0 + step):
+                    cols = slice(512 * gq, 512 * (gq + 1))
+                    nc.scalar.activation(
+                        out=e[:, cols].rearrange("p (u w) -> p u w", u=2),
+                        in_=(zl[:] if a0 and gq == 0 else z[:, cols]).rearrange("p (w u) -> p u w", u=2),
+                        func=ACT.Exp, bias=negm[:, 0:1], scale=1.0, accum_out=ssum4[:, gq : gq + 1],
+                    )
+                    for u in range(2):
+                        w0 = 256 * gq + P * u
+                        nc.tensor.transpose(pt[:, gq - g0, u, :], ew[:, w0 : w0 + P], ident_f[:])
+                eg_w = eg[:, g0 : g0 + step, :, :].bitcast(F32)
+                pt_w = pt[:, 0:step, :, :].rearrange("p g u i -> p g i u")
                 if it == NT - 1:
-                    nc.vector.tensor_copy(out=eg_w, in_=pt[:].rearrange("p u i -> p i u"))
+                    nc.vector.tensor_copy(out=eg_w, in_=pt_w)
                 else:
-                    nc.scalar.copy(out=eg_w, in_=pt[:].rearrange("p u i -> p i u"))
+                    nc.scalar.copy(out=eg_w, in_=pt_w)
             e_codes = work.tile([P, 4, P], U32, align_bytes=64)
             e_scales = work.tile([P, 4, P], U8, align_bytes=64)
             if it == NT - 1:
@@ -317,8 +321,8 @@ def tile_graphattentionlayer_kernel(tc, x, adj, aff_cropping, beta, out):
                     scales=e_scales[:].rearrange("p g i -> p (g i)"),
                     in_=eg[:].rearrange("p g i t -> p (g i t)"),
                 )
-            acc_t = pst.tile([P, 2, P], F32, tag="pt")
-            acc = acc_t[:, 0, :]
+            acc_t = pst.tile([P, 2, 2, P], F32, tag="pt")
+            acc = acc_t[:, 0, 0, :]
             for gq in range(4):
                 nc.tensor.matmul_mx(
                     out=acc,

@@ -262,10 +262,8 @@ def tile_graphattentionlayer_kernel(tc, x, adj, aff_cropping, beta, out):
             )
             negm = work.tile([P, 1], F32)
             if a0:
-                mx = work.tile([P, 2], F32)
-                nc.vector.tensor_reduce(out=mx[:, 0:1], in_=zl[:], axis=AX.X, op=ALU.max)
-                nc.vector.tensor_reduce(out=mx[:, 1:2], in_=z[:, a0:], axis=AX.X, op=ALU.max)
-                nc.vector.tensor_reduce(out=negm[:], in_=mx[:], axis=AX.X, op=ALU.max, negate=True)
+                nc.vector.tensor_reduce(out=z[:, a0 - 1 : a0], in_=zl[:], axis=AX.X, op=ALU.max)
+                nc.vector.tensor_reduce(out=negm[:], in_=z[:, a0 - 1 :], axis=AX.X, op=ALU.max, negate=True)
             else:
                 nc.vector.tensor_reduce(out=negm[:], in_=z[:], axis=AX.X, op=ALU.max, negate=True)
 

@@ -131,7 +131,33 @@ def tile_graphattentionlayer_kernel(tc, x, adj, aff_cropping, beta, out):
         pst = ctx.enter_context(tc.psum_pool(name="pst", bufs=2))
 
         panels = []
+
+        def make_w(it):
+            rows = slice(it * P, (it + 1) * P)
+            up0 = it * P
+            if it % 4 == 0 and it > 0:
+                h4 = it // 4
+                lt = psw.tile([P, 4, P], BF16, tag="w")
+                for q in range(4):
+                    nc.tensor.transpose(lt[:, q, :], cl[:, 4 * h4 + q, :], ident_b[:])
+                nc.scalar.copy(
+                    out=lw[:, 512 * h4 : 512 * (h4 + 1)], in_=lt[:].rearrange("p q i -> p (q i)")
+                )
+            panel = keep.tile([P, N - up0], F32, name="panel%d" % it)
+            panels.append(panel)
+            for c in range(it // 4, 4):
+                c0 = max(512 * c, up0)
+                c1 = 512 * (c + 1)
+                w = psw.tile([P, 512], F32, tag="w")
+                nc.tensor.matmul(
+                    out=w[:, : c1 - c0], lhsT=lw[:, rows], rhs=rw[:, c0:c1], start=True, stop=True
+                )
+                nc.scalar.copy(out=panel[:, c0 - up0 : c1 - up0], in_=w[:, : c1 - c0])
+
+        make_w(0)
         for it in range(NT):
+            if it + 1 < NT:
+                make_w(it + 1)
             rows = slice(it * P, (it + 1) * P)
             up0 = it * P
             adj_t = adjpool.tile([P, N], BF16)
@@ -162,24 +188,7 @@ def tile_graphattentionlayer_kernel(tc, x, adj, aff_cropping, beta, out):
                     bias=-10.0 * BIG, scale=10.0 * BIG,
                 )
 
-            if it % 4 == 2 and it < 12:
-                h4 = it // 4 + 1
-                lt = psw.tile([P, 4, P], BF16, tag="w")
-                for q in range(4):
-                    nc.tensor.transpose(lt[:, q, :], cl[:, 4 * h4 + q, :], ident_b[:])
-                nc.scalar.copy(
-                    out=lw[:, 512 * h4 : 512 * (h4 + 1)], in_=lt[:].rearrange("p q i -> p (q i)")
-                )
-            panel = keep.tile([P, N - up0], F32, name="panel%d" % it)
-            panels.append(panel)
-            for c in range(it // 4, 4):
-                c0 = max(512 * c, up0)
-                c1 = 512 * (c + 1)
-                w = psw.tile([P, 512], F32, tag="w")
-                nc.tensor.matmul(
-                    out=w[:, : c1 - c0], lhsT=lw[:, rows], rhs=rw[:, c0:c1], start=True, stop=True
-                )
-                nc.scalar.copy(out=panel[:, c0 - up0 : c1 - up0], in_=w[:, : c1 - c0])
+            panel = panels[it]
 
             z = work.tile([P, N], F32)
             gts = {}

from contextlib import ExitStack

import concourse.bass as bass
import concourse.mybir as mybir
import concourse.tile as tile
from concourse.masks import make_identity

F32 = mybir.dt.float32
BF16 = mybir.dt.bfloat16
U32 = mybir.dt.uint32
U8 = mybir.dt.uint8
FP8X4 = mybir.dt.float8_e4m3fn_x4
ALU = mybir.AluOpType
ACT = mybir.ActivationFunctionType
AX = mybir.AxisListType

N = 2048
D = 128
P = 128
NT = N // P
FLOPS = 2 * 2 * N * N * D
EPS = 1.0e-7
BIG = 1.0e9
HUGE = 1.0e20


def tile_graphattentionlayer_kernel(tc, x, adj, aff_cropping, beta, out):
    nc = tc.nc
    with ExitStack() as ctx:
        const = ctx.enter_context(tc.tile_pool(name="const", bufs=1))
        adjpool = ctx.enter_context(tc.tile_pool(name="adjpool", bufs=7))
        io = ctx.enter_context(tc.tile_pool(name="io", bufs=4))
        ampool = ctx.enter_context(tc.tile_pool(name="ampool", bufs=9))
        work = ctx.enter_context(tc.tile_pool(name="work", bufs=2))
        keep = ctx.enter_context(tc.tile_pool(name="keep", bufs=1))
        tbpool = ctx.enter_context(tc.tile_pool(name="tbpool", bufs=3))
        warm = const.tile([P, 1], F32)
        nc.vector.memset(warm[:], 1.0)
        nc.scalar.activation(out=warm[:], in_=warm[:], func=ACT.Sqrt)
        minus1 = const.tile([P, 1], F32)
        nc.gpsimd.memset(minus1[:], -1.0)
        ident_b = const.tile([P, P], BF16)
        make_identity(nc, ident_b[:])
        ident_f = const.tile([P, P], F32)
        make_identity(nc, ident_f[:])

        xn = const.tile([P, NT, D], BF16)
        x_rows = x.rearrange("(b p) d -> p b d", p=P)
        nc.sync.dma_start(out=xn[:, 0:8, :], in_=x_rows[:, 0:8, :])
        nc.scalar.dma_start(out=xn[:, 8:NT, :], in_=x_rows[:, 8:NT, :])
        beta_b = const.tile([P, 1], BF16)
        nc.sync.dma_start(out=beta_b[:], in_=beta.partition_broadcast(P))
        beta4 = const.tile([P, 1], F32)
        nc.vector.tensor_scalar_mul(out=beta4[:], in0=beta_b[:], scalar1=4.0)

        xT = const.tile([P, N], BF16)
        lw = const.tile([P, N], BF16)
        rw = const.tile([P, N], BF16)
        x_codes = const.tile([P, 4, D], U32, align_bytes=64)
        cl = const.tile([P, NT, P], BF16)
        nc.gpsimd.memset(cl[:], 0.0)
        x_scales = const.tile([P, 4, D], U8, align_bytes=64)

        with tc.tile_pool(name="setup", bufs=1) as setup, tc.psum_pool(name="ps_setup", bufs=4) as pss:
            cr = setup.tile([P, NT, P], BF16)
            nc.gpsimd.memset(cr[:], 0.0)
            for h in range(4):
                pt = pss.tile([P, 4, P], BF16)
                for q in range(4):
                    nc.tensor.transpose(pt[:, q, :], xn[:, 4 * h + q, :], ident_b[:])
                nc.scalar.copy(
                    out=xT[:, 512 * h : 512 * (h + 1)], in_=pt[:].rearrange("p q i -> p (q i)")
                )
            sq = setup.tile([P, NT, D], F32)
            n2 = setup.tile([P, NT], F32)
            n0 = setup.tile([P, NT], F32)
            rn0 = setup.tile([P, NT], F32)
            n1 = setup.tile([P, NT], F32)
            nc.vector.tensor_tensor(out=sq[:, 0:8, :], in0=xn[:, 0:8, :], in1=xn[:, 0:8, :], op=ALU.mult)
            nc.vector.tensor_reduce(out=n2[:, 0:8], in_=sq[:, 0:8, :], axis=AX.X, op=ALU.add)
            for b in range(8, NT):
                nc.scalar.activation(
                    out=sq[:, b, :], in_=xn[:, b, :], func=ACT.Square, accum_out=n2[:, b : b + 1]
                )
            nc.vector.tensor_scalar_max(out=n2[:], in0=n2[:], scalar1=1.0e-20)
            nc.scalar.activation(out=n0[:], in_=n2[:], func=ACT.Sqrt)
            nc.vector.reciprocal(out=rn0[:], in_=n0[:])
            nc.vector.tensor_tensor(out=n1[:], in0=n2[:], in1=rn0[:], op=ALU.mult)
            nc.vector.tensor_tensor(out=n1[:], in0=n1[:], in1=n0[:], op=ALU.add)
            fac = setup.tile([P, 4, NT], F32)
            s, r, v, qq = (fac[:, j, :] for j in range(4))
            nc.vector.reciprocal(out=r, in_=n1[:])
            nc.vector.tensor_scalar(out=s, in0=r, scalar1=beta4[:, 0:1], scalar2=None, op0=ALU.mult)
            nc.vector.tensor_tensor(out=qq, in0=r, in1=r, op=ALU.mult)
            nc.vector.scalar_tensor_tensor(out=v, in0=s, scalar=-4.0 * EPS, in1=r, op0=ALU.mult, op1=ALU.mult)
            pcs = setup.tile([P, 3, 4, NT], BF16)
            d1 = setup.tile([P, 4, NT], F32)
            d2 = setup.tile([P, 4, NT], F32)
            nc.vector.tensor_copy(out=pcs[:, 0, :, :], in_=fac[:])
            nc.vector.tensor_tensor(out=d1[:], in0=fac[:], in1=pcs[:, 0, :, :], op=ALU.subtract)
            nc.vector.tensor_copy(out=pcs[:, 1, :, :], in_=d1[:])
            nc.vector.tensor_tensor(out=d2[:], in0=d1[:], in1=pcs[:, 1, :, :], op=ALU.subtract)
            nc.vector.tensor_copy(out=pcs[:, 2, :, :], in_=d2[:])
            for dst, j, left in ((cl, 0, True), (cr, 1, False), (cl, 2, True), (cr, 3, False)):
                k0, pn = (0, 3) if j < 2 else (9, 2)
                piece = pcs[:, 0:pn, j, :].rearrange("p a b -> p b a")
                if left:
                    piece = piece.unsqueeze(3).to_broadcast([P, NT, pn, pn])
                else:
                    piece = piece.unsqueeze(2).to_broadcast([P, NT, pn, pn])
                nc.vector.tensor_copy(
                    out=dst[:, :, k0 : k0 + pn * pn].rearrange("p b (a c) -> p b a c", c=pn), in_=piece
                )
            for h in range(5):
                src, dst, h4 = (cl, lw, 0) if h == 0 else (cr, rw, h - 1)
                pt = pss.tile([P, 4, P], BF16)
                for q in range(4):
                    nc.tensor.transpose(pt[:, q, :], src[:, 4 * h4 + q, :], ident_b[:])
                if h % 2 == 0:
                    nc.vector.tensor_copy(
                        out=dst[:, 512 * h4 : 512 * (h4 + 1)], in_=pt[:].rearrange("p q i -> p (q i)")
                    )
                else:
                    nc.scalar.copy(
                        out=dst[:, 512 * h4 : 512 * (h4 + 1)], in_=pt[:].rearrange("p q i -> p (q i)")
                    )

        psg = ctx.enter_context(tc.psum_pool(name="psg", bufs=2))
        psz = ctx.enter_context(tc.psum_pool(name="psz", bufs=2))
        psw = ctx.enter_context(tc.psum_pool(name="psw", bufs=2))
        pst = ctx.enter_context(tc.psum_pool(name="pst", bufs=2))

        panels = []

        def make_w(it):
            rows = slice(it * P, (it + 1) * P)
            up0 = it * P
            if it % 4 == 0 and it > 0:
                h4 = it // 4
                lt = psw.tile([P, 4, P], BF16, tag="w")
                for q in range(4):
                    nc.tensor.transpose(lt[:, q, :], cl[:, 4 * h4 + q, :], ident_b[:])
                nc.scalar.copy(
                    out=lw[:, 512 * h4 : 512 * (h4 + 1)], in_=lt[:].rearrange("p q i -> p (q i)")
                )
            panel = keep.tile([P, N - up0], F32, name="panel%d" % it)
            panels.append(panel)
            for c in range(it // 4, 4):
                c0 = max(512 * c, up0)
                c1 = 512 * (c + 1)
                w = psw.tile([P, 512], F32, tag="w")
                nc.tensor.matmul(
                    out=w[:, : c1 - c0], lhsT=lw[:, rows], rhs=rw[:, c0:c1], start=True, stop=True
                )
                nc.scalar.copy(out=panel[:, c0 - up0 : c1 - up0], in_=w[:, : c1 - c0])

        make_w(0)
        for it in range(NT):
            if it + 1 < NT:
                make_w(it + 1)
            rows = slice(it * P, (it + 1) * P)
            up0 = it * P
            adj_t = adjpool.tile([P, N], BF16)
            nc.sync.dma_start(out=adj_t[:], in_=adj[rows, :])
            aff_t = io.tile([P, N], BF16)
            nc.sync.dma_start(out=aff_t[:], in_=aff_cropping[rows, :])

            a0 = 512 if it >= 4 else 0
            am = ampool.tile([P, N], BF16)
            if it < 4:
                nc.vector.tensor_scalar(
                    out=am[:, a0:], in0=aff_t[:, a0:], scalar1=BIG, scalar2=-BIG, op0=ALU.mult, op1=ALU.add
                )
            else:
                nc.scalar.activation(out=am[:, a0:], in_=aff_t[:, a0:], func=ACT.Copy, bias=-BIG, scale=BIG)
            nc.vector.tensor_tensor(out=am[:, a0:], in0=adj_t[:, a0:], in1=am[:, a0:], op=ALU.add)
            if a0:
                bt = psw.tile([P, 2, 4, P], BF16, tag="w")
                for j, src in enumerate((adj_t, aff_t)):
                    for q in range(4):
                        nc.tensor.transpose(bt[:, j, q, :], src[:, q * P : (q + 1) * P], ident_b[:])
                tb = tbpool.tile([P, 2, 512], F32)
                nc.scalar.activation(
                    out=tb[:, 0, :], in_=bt[:, 0, :, :].rearrange("p q i -> p (q i)"), func=ACT.Copy, scale=10.0
                )
                nc.scalar.activation(
                    out=tb[:, 1, :], in_=bt[:, 1, :, :].rearrange("p q i -> p (q i)"), func=ACT.Copy,
                    bias=-10.0 * BIG, scale=10.0 * BIG,
                )

            panel = panels[it]

            z = work.tile([P, N], F32)
            gts = {}

            def fill(c):
                nlow = min(max(it - 4 * c, 0), 4)
                lo = nlow * P
                g = psg.tile([P, 512], F32, name="g")
                for q in range(nlow):
                    jb = 4 * c + q
                    nc.tensor.transpose(
                        g[:, q * P : (q + 1) * P],
                        panels[jb][:, (it - jb) * P : (it - jb + 1) * P],
                        ident_f[:],
                    )
                if nlow < 4:
                    nc.tensor.matmul(
                        out=g[:, lo:], lhsT=xT[:, rows], rhs=xT[:, 512 * c + lo : 512 * (c + 1)],
                        start=True, stop=True,
                    )
                gts[c] = g

            def seg_of(c):
                lo = min(max(it - 4 * c, 0), 4) * P
                return panel[:, 512 * c + lo - up0 : 512 * (c + 1) - up0], lo

            def op_y(c):
                seg, lo = seg_of(c)
                nc.vector.tensor_tensor(out=seg, in0=gts[c][:, lo:], in1=seg, op=ALU.mult)

            def op_s(c):
                seg, lo = seg_of(c)
                nc.vector.scalar_tensor_tensor(
                    out=seg, in0=gts[c][:, lo:], scalar=HUGE, in1=seg, op0=ALU.mult, op1=ALU.min
                )

            def op_low(c):
                lo = min(max(it - 4 * c, 0), 4) * P
                nc.vector.scalar_tensor_tensor(
                    out=z[:, 512 * c : 512 * c + lo], in0=am[:, 512 * c : 512 * c + lo], scalar=10.0,
                    in1=gts[c][:, :lo], op0=ALU.mult, op1=ALU.add,
                )

            if a0:
                zl = psz.tile([P, 512], F32)
                for q in range(4):
                    blk = slice(q * P, (q + 1) * P)
                    srcs = (panels[q][:, (it - q) * P : (it - q + 1) * P], tb[:, 0, blk], tb[:, 1, blk])
                    for k, src in enumerate(srcs):
                        nc.tensor.matmul(
                            out=zl[:, blk], lhsT=src, rhs=ident_f[:], is_transpose=True,
                            start=(k == 0), stop=(k == 2),
                        )
            cb = it // 4
            ups = list(range(cb, 4))
            lows = list(range(a0 // 512, cb + 1 if it % 4 else cb))
            fill(ups[0])
            if len(ups) > 1:
                fill(ups[1])
            op_y(ups[0])
            for k in range(1, len(ups)):
                op_y(ups[k])
                op_s(ups[k - 1])
                if ups[k - 1] in lows:
                    op_low(ups[k - 1])
                if k + 1 < len(ups):
                    fill(ups[k + 1])
            rest = [c for c in lows if c not in ups]
            if rest:
                fill(rest[0])
                op_low(rest[0])
            op_s(ups[-1])
            if ups[-1] in lows:
                op_low(ups[-1])
            for c in rest[1:]:
                fill(c)
                op_low(c)
            nc.vector.scalar_tensor_tensor(
                out=z[:, up0:], in0=am[:, up0:], scalar=10.0, in1=panel[:], op0=ALU.mult, op1=ALU.add
            )
            negm = work.tile([P, 1], F32)
            if a0:
                nc.vector.tensor_reduce(out=z[:, a0 - 1 : a0], in_=zl[:], axis=AX.X, op=ALU.max)
                nc.vector.tensor_reduce(out=negm[:], in_=z[:, a0 - 1 :], axis=AX.X, op=ALU.max, negate=True)
            else:
                nc.vector.tensor_reduce(out=negm[:], in_=z[:], axis=AX.X, op=ALU.max, negate=True)

            if it == 0:
                xq = work.tile([P, 4, 4, D], BF16, tag="e")
                nc.sync.dma_start(out=xq[:], in_=x.rearrange("(g p t) d -> p g t d", p=P, t=4))
                xg = work.tile([P, 4, D, 4], BF16, tag="eg", align_bytes=64)
                for gq in range(4):
                    nc.scalar.copy(
                        out=xg[:, gq, :, :].rearrange("p d (u v) -> p d u v", u=2),
                        in_=xq[:, gq, :, :].rearrange("p (v u) d -> p d u v", u=2),
                    )
                nc.vector.quantize_mx(
                    out=x_codes[:].rearrange("p g d -> p (g d)").bitcast(FP8X4),
                    scales=x_scales[:].rearrange("p g d -> p (g d)"),
                    in_=xg[:].rearrange("p g d t -> p (g d t)"),
                )
            e = work.tile([P, N], BF16, tag="e")
            ssum4 = work.tile([P, 4], F32)
            eg = work.tile([P, 4, P, 4], BF16, tag="eg", align_bytes=64)
            ew = e[:].bitcast(F32)
            step = 1 if it == NT - 1 else 2
            for g0 in range(0, 4, step):
                pt = pst.tile([P, 2, 2, P], F32, tag="pt")
                for gq in range(g0, g0 + step):
                    cols = slice(512 * gq, 512 * (gq + 1))
                    nc.scalar.activation(
                        out=e[:, cols].rearrange("p (u w) -> p u w", u=2),
                        in_=(zl[:] if a0 and gq == 0 else z[:, cols]).rearrange("p (w u) -> p u w", u=2),
                        func=ACT.Exp, bias=negm[:, 0:1], scale=1.0, accum_out=ssum4[:, gq : gq + 1],
                    )
                    for u in range(2):
                        w0 = 256 * gq + P * u
                        nc.tensor.transpose(pt[:, gq - g0, u, :], ew[:, w0 : w0 + P], ident_f[:])
                eg_w = eg[:, g0 : g0 + step, :, :].bitcast(F32)
                pt_w = pt[:, 0:step, :, :].rearrange("p g u i -> p g i u")
                if it == NT - 1:
                    nc.vector.tensor_copy(out=eg_w, in_=pt_w)
                else:
                    nc.scalar.copy(out=eg_w, in_=pt_w)
            e_codes = work.tile([P, 4, P], U32, align_bytes=64)
            e_scales = work.tile([P, 4, P], U8, align_bytes=64)
            if it == NT - 1:
                for gq in range(4):
                    nc.vector.quantize_mx(
                        out=e_codes[:, gq, :].bitcast(FP8X4),
                        scales=e_scales[:, gq, :],
                        in_=eg[:, gq, :, :].rearrange("p i t -> p (i t)"),
                    )
            else:
                nc.vector.quantize_mx(
                    out=e_codes[:].rearrange("p g i -> p (g i)").bitcast(FP8X4),
                    scales=e_scales[:].rearrange("p g i -> p (g i)"),
                    in_=eg[:].rearrange("p g i t -> p (g i t)"),
                )
            acc_t = pst.tile([P, 2, 2, P], F32, tag="pt")
            acc = acc_t[:, 0, 0, :]
            for gq in range(4):
                nc.tensor.matmul_mx(
                    out=acc,
                    lhsT=e_codes[:, gq, :].bitcast(FP8X4),
                    lhsT_scale=e_scales[:, gq, :],
                    rhs=x_codes[:, gq, :].bitcast(FP8X4),
                    rhs_scale=x_scales[:, gq, :],
                    start=(gq == 0),
                    stop=(gq == 3),
                )
            ssum = work.tile([P, 1], F32)
            sjunk = work.tile([P, 4], F32)
            nc.scalar.activation(out=sjunk[:], in_=ssum4[:], func=ACT.Copy, accum_out=ssum[:, 0:1])
            rs = work.tile([P, 1], F32)
            nc.gpsimd.tensor_tensor(out=rs[:], in0=ssum[:], in1=minus1[:], op=ALU.pow)
            o = work.tile([P, D], F32)
            nc.scalar.activation(out=o[:], in_=acc, func=ACT.Copy, scale=rs[:, 0:1])
            nc.sync.dma_start(out=out[rows, :], in_=o[:])
